import numpy as np
import ml_dtypes


def mxq(x, axis, fmt="e4m3"):
    dtype, down = {"e4m3": (ml_dtypes.float8_e4m3fn, 7), "e5m2": (ml_dtypes.float8_e5m2, 14)}[fmt]
    v = np.moveaxis(np.asarray(x, np.float32).astype(ml_dtypes.bfloat16).astype(np.float64), axis, -1)
    blocks = v.reshape(v.shape[:-1] + (-1, 32))
    amax = np.abs(blocks).max(-1, keepdims=True)
    byte = np.maximum(np.where(amax > 0, np.frexp(amax)[1] - 1 + 127, 0) - down, 1)
    scale = np.exp2(byte - 127.0)
    codes = (blocks / scale).astype(np.float32).astype(dtype).astype(np.float64)
    return np.moveaxis((codes * scale).reshape(v.shape), -1, axis)


WIDE = False


def mx_kscale(k):
    if not WIDE:
        return np.ones(k)
    levels = np.array([10, -10, 5, -5, 0])
    if k % 512:
        return np.exp2(np.random.permutation(np.resize(levels, k // 32))).repeat(32)
    a = np.empty((k // 512, 16))
    for p in range(k // 512):
        a[p, :8] = np.random.permutation(np.resize(levels, 8))
        for g in range(8):
            far = levels[np.abs(levels - a[p, g]) >= 10]
            a[p, g + 8] = far[np.random.randint(len(far))]
    return np.exp2(a.ravel()).repeat(32)


BF16 = ml_dtypes.bfloat16


def bf(x):
    return np.asarray(x, np.float32).astype(BF16)


def f64(x):
    return np.asarray(x).astype(np.float64)


E2M1 = np.array([0.0, 0.5, 1.0, 1.5, 2.0, 3.0, 4.0, 6.0, -0.0, -0.5, -1.0, -1.5, -2.0, -3.0, -4.0, -6.0])


def pack_weight(w, fmt):
    k, n = w.shape
    w = f64(bf(w)).reshape(k // 32, 32, n)
    amax = np.abs(w).max(1)
    if fmt == "e4m3":
        byte = np.frexp(amax)[1] - 1 + 127 - 7
    else:
        mant, ex = np.frexp(amax / 6.0)
        byte = np.where(mant > 0.5, ex, ex - 1) + 127
    byte = np.clip(np.where(amax > 0, byte, 1), 1, 254)
    scaled = (w * np.exp2(127.0 - byte)[:, None, :]).reshape(k, n).astype(np.float32)
    by_word = np.ascontiguousarray(scaled.reshape(k // 512, 128, 4, n).transpose(0, 1, 3, 2))
    if fmt == "e4m3":
        words = by_word.astype(ml_dtypes.float8_e4m3fn).view(np.uint8)
    else:
        c = by_word.astype(ml_dtypes.float4_e2m1fn).view(np.uint8) & 0xF
        words = c[..., 0::2] | (c[..., 1::2] << 4)
    return np.ascontiguousarray(words), np.ascontiguousarray(byte.astype(np.uint8).reshape(k // 512, 16, n))


def unpack_weight(words, scales, fmt):
    g, p, n, _ = words.shape
    if fmt == "e4m3":
        vals = np.ascontiguousarray(words).view(ml_dtypes.float8_e4m3fn).astype(np.float64)
    else:
        nib = np.empty((g, p, n, 4), np.uint8)
        nib[..., 0::2] = words & 0xF
        nib[..., 1::2] = words >> 4
        vals = E2M1[nib]
    vals = vals * np.repeat(np.exp2(scales.astype(np.float64) - 127.0), 8, axis=1)[..., None]
    return vals.transpose(0, 1, 3, 2).reshape(g * 512, n)
def pack4(w):
    words, scales = pack_weight(w, "e2m1")
    return words.reshape(words.shape[0], 128, -1), scales


def unpack4(words, scales):
    return unpack_weight(words.reshape(words.shape[0], 128, -1, 2), scales, "e2m1")


E, F, H, MID, OUT = 4096, 64, 192, 1024, 256
D = 2 * (F + H)
IN = D + 1


def draw0():
    s = mx_kscale(D)
    t = mx_kscale(MID)
    w1 = np.concatenate([np.random.standard_normal((MID, D)) / np.sqrt(D) / s[None, :],
                         np.random.standard_normal((MID, 1)) * 0.5], axis=1) * t[:, None]
    inputs = {"dst_node_feat": bf(np.random.standard_normal((E, F)) * s[:F]),
              "dst_node_hidden": bf(np.random.standard_normal((E, H)) * s[F:F + H]),
              "src_node_feat": bf(np.random.standard_normal((E, F)) * s[F + H:2 * F + H]),
              "src_node_hidden": bf(np.random.standard_normal((E, H)) * s[2 * F + H:]),
              "edge_feat": bf(np.random.standard_normal(E)),
              "W1": bf(w1),
              "b1": bf(np.random.standard_normal(MID) * 0.3 * t)}
    w2 = np.random.standard_normal((OUT, MID)) / np.sqrt(MID) / t[None, :]
    inputs["W2_words"], inputs["W2_scales"] = pack4(w2.T)
    inputs["b2"] = bf(np.random.standard_normal(OUT) * 0.3)
    return inputs


def core(dst_node_feat, dst_node_hidden, src_node_feat, src_node_hidden, edge_feat, W1, b1, W2_words, W2_scales, b2):
    x = np.concatenate([f64(dst_node_feat), f64(dst_node_hidden), f64(src_node_feat), f64(src_node_hidden),
                        f64(edge_feat)[:, None]], axis=1)
    w1 = f64(W1)
    pre = (mxq(x[:, :D], 1, "e4m3") @ mxq(w1[:, :D], 1, "e4m3").T) + x[:, D:] * w1[:, D] + f64(b1)
    h = np.maximum(pre, 0.0)
    return np.tanh((mxq(h, 1, "e4m3") @ unpack4(W2_words, W2_scales)) + f64(b2))


def e4m3fn_bytes(y):
    return np.clip(np.asarray(y, np.float64), -448.0, 448.0).astype(np.float32).astype(ml_dtypes.float8_e4m3fn).view(np.uint8)


def e4m3fn_values(b):
    return np.asarray(b, np.uint8).view(ml_dtypes.float8_e4m3fn).astype(np.float64)


def setup_inputs():
    d = draw0()
    x0 = np.asarray(d['src_node_hidden']).astype(np.float64)
    s = (np.max(np.abs(x0), axis=(0,), keepdims=True) / 448.0).astype(np.float32)
    out = {}
    for k, v in d.items():
        if k == 'src_node_hidden':
            out['src_node_hidden_bytes'] = e4m3fn_bytes(x0 / s.astype(np.float64))
            out['src_node_hidden_scale'] = s
        else:
            out[k] = v
    return out


def reference(dst_node_feat, dst_node_hidden, src_node_feat, src_node_hidden_bytes, src_node_hidden_scale, edge_feat, W1, b1, W2_words, W2_scales, b2):
    return core(dst_node_feat, dst_node_hidden, src_node_feat, e4m3fn_values(src_node_hidden_bytes) * src_node_hidden_scale.astype(np.float64), edge_feat, W1, b1, W2_words, W2_scales, b2)

@@ -1,0 +1,314 @@
+from contextlib import ExitStack
+
+import concourse.mybir as mybir
+from concourse.masks import make_identity
+
+E, F, H, MID, OUT = 4096, 64, 192, 1024, 256
+D = 2 * (F + H)
+
+F32 = mybir.dt.float32
+BF16 = mybir.dt.bfloat16
+I32 = mybir.dt.int32
+U32 = mybir.dt.uint32
+U8 = mybir.dt.uint8
+FP8 = mybir.dt.float8_e4m3fn
+FP8X4 = mybir.dt.float8_e4m3fn_x4
+FP4X4 = mybir.dt.float4_e2m1fn_x4
+ALU = mybir.AluOpType
+ACT = mybir.ActivationFunctionType
+
+FLOPS = 2 * E * (MID * (D + 1) + MID * OUT)
+
+P = 128
+T = 4
+G = MID // 512
+NE = 512
+CH = E // NE
+R = NE // P
+Q = NE // P
+OT = OUT // P
+
+
+def tile_edgenetwork_t_w4_kernel(tc, dst_feat, dst_hidden, src_feat, src_bytes, src_scale, edge_feat, W1, b1, W2_words, W2_scales, b2, out):
+    nc = tc.nc
+    with ExitStack() as ctx:
+        keep = ctx.enter_context(tc.tile_pool(name="keep", bufs=1))
+        xin = ctx.enter_context(tc.tile_pool(name="xin", bufs=CH))
+        work = ctx.enter_context(tc.tile_pool(name="work", bufs=3))
+        psum = ctx.enter_context(tc.psum_pool(name="psum", bufs=2))
+        ctx.enter_context(tc.manual_schedule())
+
+        ident = keep.tile([P, P], F32)
+        sc_bc = keep.tile([P, H], F32)
+        e_bc = keep.tile([P, E], BF16)
+        b1c = keep.tile([P, G, T], BF16)
+        b2c = [keep.tile([P, 2], BF16, name="b2c%d" % ot) for ot in range(OT)]
+        w32 = keep.tile([P, G, T], F32)
+        dummy = keep.tile([P, 1], F32)
+        w_codes = keep.tile([P, G, T, P], U32, align_bytes=64)
+        w_scales = keep.tile([P, G, T, P], U8, align_bytes=64)
+        w2 = keep.tile([P, G, 2 * OUT], U8, align_bytes=64)
+        w2s = keep.tile([P, G, OUT], U8, align_bytes=64)
+        w_raw = [keep.tile([P, T, D + 2], BF16, name="w_raw%d" % g) for g in range(G)]
+
+        x_row = {}
+        x_byt = {}
+
+        def load_x(c):
+            xr = xin.tile([P, R, D], BF16, name="xr")
+            xb = xin.tile([P, R, H], U8, name="xb")
+            nc.sync.dma_start(out=xb[:], in_=src_bytes.rearrange("(c j r) f -> c j r f", j=P, r=R)[c])
+            nc.sync.dma_start(out=xr[:, :, F : F + H], in_=dst_hidden.rearrange("(c j r) f -> c j r f", j=P, r=R)[c])
+            nc.sync.dma_start(out=xr[:, :, 0:F], in_=dst_feat.rearrange("(c j r) f -> c j r f", j=P, r=R)[c])
+            nc.sync.dma_start(out=xr[:, :, F + H : 2 * F + H], in_=src_feat.rearrange("(c j r) f -> c j r f", j=P, r=R)[c])
+            x_row[c] = xr
+            x_byt[c] = xb
+
+        def load_w1(g):
+            nc.sync.dma_start(out=w_raw[g][:, :, 0 : D + 1], in_=W1.rearrange("(g m t) k -> g m t k", g=G, t=T)[g])
+
+        def load_e(c0, c1):
+            nc.scalar.dma_start(out=e_bc[:, c0 * NE : c1 * NE], in_=edge_feat[c0 * NE : c1 * NE].partition_broadcast(P))
+
+        nc.vector.memset(dummy[:], 0.0)
+        nc.vector.memset(w2s[:].rearrange("p g n -> p (g n)").bitcast(I32), 0)
+        make_identity(nc, ident[:])
+        nc.scalar.dma_start(out=sc_bc[:], in_=src_scale.rearrange("o k -> (o k)").partition_broadcast(P))
+        load_e(0, 1)
+        nc.scalar.dma_start(out=b1c[:], in_=b1.rearrange("(g m t) -> m g t", g=G, t=T))
+        load_x(0)
+        load_w1(0)
+        load_x(1)
+        load_w1(1)
+        nc.scalar.activation(out=dummy[:], in_=dummy[:], func=ACT.Tanh)
+        load_e(1, 4)
+        load_e(4, CH)
+        nc.sync.dma_start(out=w2[:], in_=W2_words.rearrange("g p n -> p g n"))
+        for qd in range(4):
+            nc.sync.dma_start(
+                out=w2s[32 * qd : 32 * qd + 4, :, :].bitcast(I32),
+                in_=W2_scales[:, 4 * qd : 4 * qd + 4, :].rearrange("g q n -> q g n").bitcast(I32),
+            )
+        with nc.allow_non_contiguous_dma(reason="256 bias values, one to a partition"):
+            for ot in range(OT):
+                nc.sync.dma_start(out=b2c[ot][:, 0:1], in_=b2.rearrange("(t p o) -> t p o", t=OT, o=1)[ot])
+        for c in range(2, CH):
+            load_x(c)
+
+        def widen(c):
+            for r in range(R):
+                nc.vector.tensor_tensor(
+                    out=x_row[c][:, r, 2 * F + H : D],
+                    in0=x_byt[c][:, r, :].bitcast(FP8),
+                    in1=sc_bc[:],
+                    op=ALU.mult,
+                )
+
+        x_grp = {}
+        x_tp = {}
+        x_q = {}
+
+        def tp_x(c, rh):
+            tp = psum.tile([P, 4, P], F32, name="tp")
+            words = x_row[c][:].rearrange("p r k -> p (r k)").bitcast(F32)
+            for r2 in range(2):
+                r = 2 * rh + r2
+                for u in range(2):
+                    nc.tensor.transpose(tp[:, 2 * r2 + u, :], words[:, 256 * r + u : 256 * (r + 1) : 2], ident[:])
+            x_tp[c, rh] = tp
+
+        def exit_x(c, rh):
+            if rh == 0:
+                xg = work.tile([P, NE * T], BF16, name="xg", bufs=2, align_bytes=64)
+                x_grp[c] = xg
+            dst = x_grp[c][:].bitcast(F32).rearrange("p (j h w) -> p j h w", h=2, w=4)[:, :, rh, :]
+            nc.scalar.copy(out=dst, in_=x_tp[c, rh][:].rearrange("p w j -> p j w"))
+
+        def quant_x(c):
+            xc = work.tile([P, NE], U32, name="xc", bufs=2, align_bytes=64)
+            xs = work.tile([P, NE], U8, name="xs", bufs=2, align_bytes=64)
+            nc.vector.quantize_mx(out=xc[:].bitcast(FP8X4), scales=xs[:], in_=x_grp[c][:])
+            x_q[c] = (xc, xs)
+
+        w_grp = {}
+
+        def prep_w(g):
+            wg = work.tile([P, T * P * 4], BF16, name="wg", bufs=2, align_bytes=64)
+            words = w_raw[g][:].rearrange("p t k -> p (t k)").bitcast(F32)
+            pitch = (D + 2) // 2
+            for h in range(2):
+                tp = psum.tile([P, 4, P], F32, name="tp")
+                for t2 in range(2):
+                    for u in range(2):
+                        base = pitch * (2 * h + t2)
+                        nc.tensor.transpose(tp[:, 2 * t2 + u, :], words[:, base + u : base + 256 : 2], ident[:])
+                dst = wg[:].bitcast(F32).rearrange("p (t m u) -> p t m u", t=T, u=2)[:, 2 * h : 2 * h + 2, :, :]
+                nc.vector.tensor_copy(out=dst, in_=tp[:].rearrange("p (t u) m -> p t m u", u=2))
+            w_grp[g] = wg
+
+        def quant_w(g):
+            nc.vector.quantize_mx(
+                out=w_codes[:, g, :, :].rearrange("p t m -> p (t m)").bitcast(FP8X4),
+                scales=w_scales[:, g, :, :].rearrange("p t m -> p (t m)"),
+                in_=w_grp[g][:],
+            )
+
+        t_tile = {}
+
+        def make_t(c, g, t):
+            if t == 0:
+                tt = work.tile([P, T, NE], F32, name="tt")
+                t_tile[c, g] = tt
+            nc.scalar.activation(
+                out=t_tile[c, g][:, t, :],
+                in_=e_bc[:, c * NE : (c + 1) * NE],
+                func=ACT.Identity,
+                bias=b1c[:, g, t : t + 1],
+                scale=w32[:, g, t : t + 1],
+            )
+
+        h_tile = {}
+        h_q = {}
+
+        def mm_add(c, g, q):
+            if q == 0:
+                hh = work.tile([P, NE * T], BF16, name="hh", align_bytes=64)
+                h_tile[c, g] = hh
+            cols = slice(q * P, (q + 1) * P)
+            xc, xs = x_q[c]
+            acc = psum.tile([P, T, P], F32, name="acc", bufs=4)
+            for t in range(T):
+                nc.tensor.matmul_mx(
+                    out=acc[:, t, :],
+                    lhsT=w_codes[:, g, t, :].bitcast(FP8X4),
+                    lhsT_scale=w_scales[:, g, t, :],
+                    rhs=xc[:, cols].bitcast(FP8X4),
+                    rhs_scale=xs[:, cols],
+                    start=True,
+                    stop=True,
+                )
+            nc.vector.tensor_tensor(
+                out=h_tile[c, g][:, q * P * T : (q + 1) * P * T].rearrange("p (c i t) -> p c t i", i=4, t=T),
+                in0=acc[:].rearrange("p t (c i) -> p c t i", i=4),
+                in1=t_tile[c, g][:, :, cols].rearrange("p t (c i) -> p c t i", i=4),
+                op=ALU.add,
+            )
+
+        def relu(c, g):
+            hh = h_tile[c, g]
+            nc.vector.tensor_scalar(out=hh[:], in0=hh[:], scalar1=0.0, scalar2=None, op0=ALU.max)
+
+        def quant_h(c, g):
+            hc = work.tile([P, NE], U32, name="hc", bufs=4, align_bytes=64)
+            hs = work.tile([P, NE], U8, name="hs", bufs=4, align_bytes=64)
+            nc.vector.quantize_mx(out=hc[:].bitcast(FP8X4), scales=hs[:], in_=h_tile[c, g][:])
+            h_q[c, g] = (hc, hs)
+
+        y_ps = {}
+        y_sb = {}
+        o_sb = {}
+
+        def stage2(c):
+            for ot in range(OT):
+                y = psum.tile([P, NE], F32, name="y", bufs=2)
+                for g in range(G):
+                    hc, hs = h_q[c, g]
+                    nc.tensor.matmul_mx(
+                        out=y[:],
+                        lhsT=w2[:, g, 2 * P * ot : 2 * P * (ot + 1)].bitcast(FP4X4),
+                        lhsT_scale=w2s[:, g, P * ot : P * (ot + 1)],
+                        rhs=hc[:].bitcast(FP8X4),
+                        rhs_scale=hs[:],
+                        start=(g == 0),
+                        stop=(g == G - 1),
+                    )
+                y_ps[c, ot] = y
+
+        def tanh_y(c, ot):
+            ys = work.tile([P, NE], F32, name="ys", bufs=4)
+            nc.scalar.activation(out=ys[:], in_=y_ps[c, ot][:], func=ACT.Tanh, bias=b2c[ot][:, 0:1], scale=1.0)
+            y_sb[c, ot] = ys
+
+        def out_half(c, qh):
+            if qh == 0:
+                oo = work.tile([P, Q, OUT], F32, name="oo")
+                o_sb[c] = oo
+            tp = psum.tile([P, 4, P], F32, name="tp")
+            for q2 in range(2):
+                for ot in range(OT):
+                    q = 2 * qh + q2
+                    nc.tensor.transpose(tp[:, 2 * q2 + ot, :], y_sb[c, ot][:, q * P : (q + 1) * P], ident[:])
+            nc.scalar.copy(
+                out=o_sb[c][:, 2 * qh : 2 * qh + 2, :].rearrange("p q o -> p (q o)"),
+                in_=tp[:].rearrange("p w o -> p (w o)"),
+            )
+            nc.sync.dma_start(
+                out=out.rearrange("(c q p) o -> c p q o", q=Q, p=P)[c][:, 2 * qh : 2 * qh + 2, :],
+                in_=o_sb[c][:, 2 * qh : 2 * qh + 2, :],
+            )
+
+        widen(0)
+        for rh in range(2):
+            tp_x(0, rh)
+            exit_x(0, rh)
+        nc.vector.tensor_copy(out=w32[:, 0, :], in_=w_raw[0][:, :, D])
+        prep_w(0)
+        quant_x(0)
+        quant_w(0)
+        for t in range(T):
+            make_t(0, 0, t)
+        widen(1)
+        nc.vector.tensor_copy(out=w32[:, 1, :], in_=w_raw[1][:, :, D])
+        prep_w(1)
+        quant_w(1)
+
+        for c in range(CH):
+            last = c == CH - 1
+            make_t(c, 1, 0)
+            if not last:
+                tp_x(c + 1, 0)
+                tp_x(c + 1, 1)
+                exit_x(c + 1, 0)
+            make_t(c, 1, 1)
+            if not last:
+                exit_x(c + 1, 1)
+            make_t(c, 1, 2)
+            make_t(c, 1, 3)
+            for q in range(Q):
+                mm_add(c, 0, q)
+                if c > 0 and q == 1:
+                    relu(c - 1, 1)
+                if c > 0 and q == 2:
+                    quant_h(c - 1, 1)
+            if c + 2 < CH:
+                widen(c + 2)
+            if c > 1:
+                out_half(c - 2, 0)
+                out_half(c - 2, 1)
+            if not last:
+                make_t(c + 1, 0, 0)
+                make_t(c + 1, 0, 1)
+            for q in range(Q):
+                mm_add(c, 1, q)
+                if q == 0 and not last:
+                    quant_x(c + 1)
+                if q == 1:
+                    relu(c, 0)
+                if q == 2:
+                    quant_h(c, 0)
+                    if c > 0:
+                        stage2(c - 1)
+                        tanh_y(c - 1, 0)
+                        tanh_y(c - 1, 1)
+            if not last:
+                make_t(c + 1, 0, 2)
+                make_t(c + 1, 0, 3)
+        relu(CH - 1, 1)
+        out_half(CH - 2, 0)
+        quant_h(CH - 1, 1)
+        out_half(CH - 2, 1)
+        stage2(CH - 1)
+        tanh_y(CH - 1, 0)
+        tanh_y(CH - 1, 1)
+        out_half(CH - 1, 0)
+        out_half(CH - 1, 1)

@@ -27,6 +27,7 @@ CH = E // NE
 R = NE // P
 Q = NE // P
 OT = OUT // P
+W_PITCH = D + 16
 
 
 def tile_edgenetwork_t_w4_kernel(tc, dst_feat, dst_hidden, src_feat, src_bytes, src_scale, edge_feat, W1, b1, W2_words, W2_scales, b2, out):
@@ -49,7 +50,7 @@ def tile_edgenetwork_t_w4_kernel(tc, dst_feat, dst_hidden, src_feat, src_bytes, 
         w_scales = keep.tile([P, G, T, P], U8, align_bytes=64)
         w2 = keep.tile([P, G, 2 * OUT], U8, align_bytes=64)
         w2s = keep.tile([P, G, OUT], U8, align_bytes=64)
-        w_raw = [keep.tile([P, T, D + 2], BF16, name="w_raw%d" % g) for g in range(G)]
+        w_raw = [keep.tile([P, T, W_PITCH], BF16, name="w_raw%d" % g) for g in range(G)]
 
         x_row = {}
         x_byt = {}
@@ -64,25 +65,29 @@ def tile_edgenetwork_t_w4_kernel(tc, dst_feat, dst_hidden, src_feat, src_bytes, 
             x_row[c] = xr
             x_byt[c] = xb
 
-        def load_w1(g):
-            nc.sync.dma_start(out=w_raw[g][:, :, 0 : D + 1], in_=W1.rearrange("(g m t) k -> g m t k", g=G, t=T)[g])
+        def load_w1(g, t0, t1):
+            nc.sync.dma_start(
+                out=w_raw[g][:, t0:t1, 0 : D + 1],
+                in_=W1.rearrange("(g m t) k -> g m t k", g=G, t=T)[g][:, t0:t1, :],
+            )
 
-        def load_e(c0, c1):
-            nc.scalar.dma_start(out=e_bc[:, c0 * NE : c1 * NE], in_=edge_feat[c0 * NE : c1 * NE].partition_broadcast(P))
+        def load_e(engine, c0, c1):
+            engine.dma_start(out=e_bc[:, c0 * NE : c1 * NE], in_=edge_feat[c0 * NE : c1 * NE].partition_broadcast(P))
 
         nc.vector.memset(dummy[:], 0.0)
         nc.vector.memset(w2s[:].rearrange("p g n -> p (g n)").bitcast(I32), 0)
         make_identity(nc, ident[:])
-        nc.scalar.dma_start(out=sc_bc[:], in_=src_scale.rearrange("o k -> (o k)").partition_broadcast(P))
-        load_e(0, 1)
-        nc.scalar.dma_start(out=b1c[:], in_=b1.rearrange("(g m t) -> m g t", g=G, t=T))
         load_x(0)
-        load_w1(0)
-        load_x(1)
-        load_w1(1)
+        nc.scalar.dma_start(out=sc_bc[:], in_=src_scale.rearrange("o k -> (o k)").partition_broadcast(P))
+        nc.scalar.dma_start(out=b1c[:], in_=b1.rearrange("(g m t) -> m g t", g=G, t=T))
+        load_e(nc.scalar, 0, 1)
         nc.scalar.activation(out=dummy[:], in_=dummy[:], func=ACT.Tanh)
-        load_e(1, 4)
-        load_e(4, CH)
+        load_w1(0, 0, 2)
+        load_w1(0, 2, 4)
+        load_w1(1, 0, 4)
+        load_x(1)
+        load_e(nc.sync, 1, 3)
+        load_x(2)
         nc.sync.dma_start(out=w2[:], in_=W2_words.rearrange("g p n -> p g n"))
         for qd in range(4):
             nc.sync.dma_start(
@@ -92,7 +97,9 @@ def tile_edgenetwork_t_w4_kernel(tc, dst_feat, dst_hidden, src_feat, src_bytes, 
         with nc.allow_non_contiguous_dma(reason="256 bias values, one to a partition"):
             for ot in range(OT):
                 nc.sync.dma_start(out=b2c[ot][:, 0:1], in_=b2.rearrange("(t p o) -> t p o", t=OT, o=1)[ot])
-        for c in range(2, CH):
+        load_x(3)
+        load_e(nc.sync, 3, CH)
+        for c in range(4, CH):
             load_x(c)
 
         def widen(c):
@@ -132,19 +139,27 @@ def tile_edgenetwork_t_w4_kernel(tc, dst_feat, dst_hidden, src_feat, src_bytes, 
 
         w_grp = {}
 
-        def prep_w(g):
-            wg = work.tile([P, T * P * 4], BF16, name="wg", bufs=2, align_bytes=64)
+        w_tp = {}
+
+        def tp_w(g, h):
             words = w_raw[g][:].rearrange("p t k -> p (t k)").bitcast(F32)
-            pitch = (D + 2) // 2
-            for h in range(2):
-                tp = psum.tile([P, 4, P], F32, name="tp")
-                for t2 in range(2):
-                    for u in range(2):
-                        base = pitch * (2 * h + t2)
-                        nc.tensor.transpose(tp[:, 2 * t2 + u, :], words[:, base + u : base + 256 : 2], ident[:])
-                dst = wg[:].bitcast(F32).rearrange("p (t m u) -> p t m u", t=T, u=2)[:, 2 * h : 2 * h + 2, :, :]
-                nc.vector.tensor_copy(out=dst, in_=tp[:].rearrange("p (t u) m -> p t m u", u=2))
-            w_grp[g] = wg
+            pitch = W_PITCH // 2
+            tp = psum.tile([P, 4, P], F32, name="tp")
+            for t2 in range(2):
+                for u in range(2):
+                    base = pitch * (2 * h + t2)
+                    nc.tensor.transpose(tp[:, 2 * t2 + u, :], words[:, base + u : base + 256 : 2], ident[:])
+            w_tp[g, h] = tp
+
+        def exit_w(g, h, copy):
+            if h == 0:
+                wg = work.tile([P, T * P * 4], BF16, name="wg", bufs=2, align_bytes=64)
+                w_grp[g] = wg
+            dst = w_grp[g][:].bitcast(F32).rearrange("p (t m u) -> p t m u", t=T, u=2)[:, 2 * h : 2 * h + 2, :, :]
+            copy(out=dst, in_=w_tp[g, h][:].rearrange("p (t u) m -> p t m u", u=2))
+
+        def widen_w(g, t0, t1):
+            nc.vector.tensor_copy(out=w32[:, g, t0:t1], in_=w_raw[g][:, t0:t1, D])
 
         def quant_w(g):
             nc.vector.quantize_mx(
@@ -155,25 +170,32 @@ def tile_edgenetwork_t_w4_kernel(tc, dst_feat, dst_hidden, src_feat, src_bytes, 
 
         t_tile = {}
 
-        def make_t(c, g, t):
+        def make_t(c, g, t, on_vector=False):
             if t == 0:
-                tt = work.tile([P, T, NE], F32, name="tt")
+                tt = work.tile([P, T, NE], F32, name="tt", bufs=4)
                 t_tile[c, g] = tt
-            nc.scalar.activation(
-                out=t_tile[c, g][:, t, :],
-                in_=e_bc[:, c * NE : (c + 1) * NE],
-                func=ACT.Identity,
-                bias=b1c[:, g, t : t + 1],
-                scale=w32[:, g, t : t + 1],
-            )
+            if on_vector:
+                nc.vector.tensor_scalar(
+                    out=t_tile[c, g][:, t, :],
+                    in0=e_bc[:, c * NE : (c + 1) * NE],
+                    scalar1=w_raw[g][:, t, D : D + 1],
+                    scalar2=b1c[:, g, t : t + 1],
+                    op0=ALU.mult,
+                    op1=ALU.add,
+                )
+            else:
+                nc.scalar.activation(
+                    out=t_tile[c, g][:, t, :],
+                    in_=e_bc[:, c * NE : (c + 1) * NE],
+                    func=ACT.Identity,
+                    bias=b1c[:, g, t : t + 1],
+                    scale=w32[:, g, t : t + 1],
+                )
 
         h_tile = {}
         h_q = {}
 
-        def mm_add(c, g, q):
-            if q == 0:
-                hh = work.tile([P, NE * T], BF16, name="hh", align_bytes=64)
-                h_tile[c, g] = hh
+        def mm_add(c, g, q, h_out):
             cols = slice(q * P, (q + 1) * P)
             xc, xs = x_q[c]
             acc = psum.tile([P, T, P], F32, name="acc", bufs=4)
@@ -188,40 +210,60 @@ def tile_edgenetwork_t_w4_kernel(tc, dst_feat, dst_hidden, src_feat, src_bytes, 
                     stop=True,
                 )
             nc.vector.tensor_tensor(
-                out=h_tile[c, g][:, q * P * T : (q + 1) * P * T].rearrange("p (c i t) -> p c t i", i=4, t=T),
+                out=h_out.rearrange("p (c i t) -> p c t i", i=4, t=T),
                 in0=acc[:].rearrange("p t (c i) -> p c t i", i=4),
                 in1=t_tile[c, g][:, :, cols].rearrange("p t (c i) -> p c t i", i=4),
                 op=ALU.add,
             )
 
-        def relu(c, g):
-            hh = h_tile[c, g]
-            nc.vector.tensor_scalar(out=hh[:], in0=hh[:], scalar1=0.0, scalar2=None, op0=ALU.max)
+        def new_h(c):
+            hh = work.tile([P, G, NE * T], BF16, name="hh", bufs=2, align_bytes=64)
+            h_tile[c] = hh
 
-        def quant_h(c, g):
-            hc = work.tile([P, NE], U32, name="hc", bufs=4, align_bytes=64)
-            hs = work.tile([P, NE], U8, name="hs", bufs=4, align_bytes=64)
-            nc.vector.quantize_mx(out=hc[:].bitcast(FP8X4), scales=hs[:], in_=h_tile[c, g][:])
-            h_q[c, g] = (hc, hs)
+        def stage1(c, g, q):
+            mm_add(c, g, q, h_tile[c][:, g, q * P * T : (q + 1) * P * T])
+
+        def relu(h):
+            nc.vector.tensor_scalar(out=h, in0=h, scalar1=0.0, scalar2=None, op0=ALU.max)
+
+        def relu_chunk(c, split=False):
+            if split:
+                h = h_tile[c][:, 1, :]
+                nc.scalar.activation(out=h, in_=h, func=ACT.Relu)
+                relu(h_tile[c][:, 0, :])
+            else:
+                relu(h_tile[c][:].rearrange("p g w -> p (g w)"))
+
+        def quant_chunk(c):
+            hc = work.tile([P, G, NE], U32, name="hc", bufs=2, align_bytes=64)
+            hs = work.tile([P, G, NE], U8, name="hs", bufs=2, align_bytes=64)
+            h_q[c] = (hc, hs)
+            nc.vector.quantize_mx(
+                out=hc[:].rearrange("p g n -> p (g n)").bitcast(FP8X4),
+                scales=hs[:].rearrange("p g n -> p (g n)"),
+                in_=h_tile[c][:].rearrange("p g w -> p (g w)"),
+            )
 
         y_ps = {}
         y_sb = {}
-        o_sb = {}
+        o_ps = {}
+
+        def mm2(y, ot, hc, hs):
+            for g in range(G):
+                nc.tensor.matmul_mx(
+                    out=y,
+                    lhsT=w2[:, g, 2 * P * ot : 2 * P * (ot + 1)].bitcast(FP4X4),
+                    lhsT_scale=w2s[:, g, P * ot : P * (ot + 1)],
+                    rhs=hc[:, g, :].bitcast(FP8X4),
+                    rhs_scale=hs[:, g, :],
+                    start=(g == 0),
+                    stop=(g == G - 1),
+                )
 
         def stage2(c):
             for ot in range(OT):
                 y = psum.tile([P, NE], F32, name="y", bufs=2)
-                for g in range(G):
-                    hc, hs = h_q[c, g]
-                    nc.tensor.matmul_mx(
-                        out=y[:],
-                        lhsT=w2[:, g, 2 * P * ot : 2 * P * (ot + 1)].bitcast(FP4X4),
-                        lhsT_scale=w2s[:, g, P * ot : P * (ot + 1)],
-                        rhs=hc[:].bitcast(FP8X4),
-                        rhs_scale=hs[:],
-                        start=(g == 0),
-                        stop=(g == G - 1),
-                    )
+                mm2(y[:], ot, *h_q[c])
                 y_ps[c, ot] = y
 
         def tanh_y(c, ot):
@@ -229,86 +271,160 @@ def tile_edgenetwork_t_w4_kernel(tc, dst_feat, dst_hidden, src_feat, src_bytes, 
             nc.scalar.activation(out=ys[:], in_=y_ps[c, ot][:], func=ACT.Tanh, bias=b2c[ot][:, 0:1], scale=1.0)
             y_sb[c, ot] = ys
 
-        def out_half(c, qh):
-            if qh == 0:
-                oo = work.tile([P, Q, OUT], F32, name="oo")
-                o_sb[c] = oo
+        def tp_out(c, qh):
             tp = psum.tile([P, 4, P], F32, name="tp")
             for q2 in range(2):
                 for ot in range(OT):
                     q = 2 * qh + q2
                     nc.tensor.transpose(tp[:, 2 * q2 + ot, :], y_sb[c, ot][:, q * P : (q + 1) * P], ident[:])
-            nc.scalar.copy(
-                out=o_sb[c][:, 2 * qh : 2 * qh + 2, :].rearrange("p q o -> p (q o)"),
-                in_=tp[:].rearrange("p w o -> p (w o)"),
+            o_ps[c, qh] = tp
+
+        def exit_out(c, qh):
+            oo = work.tile([P, 2, OUT], F32, name="oo", bufs=4)
+            nc.scalar.copy(out=oo[:].rearrange("p q o -> p (q o)"), in_=o_ps[c, qh][:].rearrange("p w o -> p (w o)"))
+            nc.sync.dma_start(out=out.rearrange("(c q p) o -> c p q o", q=Q, p=P)[c][:, 2 * qh : 2 * qh + 2, :], in_=oo[:])
+
+        hl = {}
+        hl_q = {}
+
+        def last_stage1(q, g):
+            if g == 0:
+                hq = work.tile([P, G, P * T], BF16, name="hq", bufs=4, align_bytes=64)
+                hl[q] = hq
+            mm_add(CH - 1, g, q, hl[q][:, g, :])
+
+        def last_relu(q):
+            relu(hl[q][:].rearrange("p g w -> p (g w)"))
+
+        def last_quant(q):
+            hc = work.tile([P, G, P], U32, name="hcq", bufs=4, align_bytes=64)
+            hs = work.tile([P, G, P], U8, name="hsq", bufs=4, align_bytes=64)
+            nc.vector.quantize_mx(
+                out=hc[:].rearrange("p g n -> p (g n)").bitcast(FP8X4),
+                scales=hs[:].rearrange("p g n -> p (g n)"),
+                in_=hl[q][:].rearrange("p g w -> p (g w)"),
             )
-            nc.sync.dma_start(
-                out=out.rearrange("(c q p) o -> c p q o", q=Q, p=P)[c][:, 2 * qh : 2 * qh + 2, :],
-                in_=o_sb[c][:, 2 * qh : 2 * qh + 2, :],
-            )
+            hl_q[q] = (hc, hs)
+
+        lys = {}
+
+        def last_stage2(q):
+            y = psum.tile([P, OT, P], F32, name="y", bufs=2)
+            ys = work.tile([P, OT, P], F32, name="ysq")
+            for ot in range(OT):
+                mm2(y[:, ot, :], ot, *hl_q[q])
+            for ot in range(OT):
+                nc.scalar.activation(out=ys[:, ot, :], in_=y[:, ot, :], func=ACT.Tanh, bias=b2c[ot][:, 0:1], scale=1.0)
+            lys[q] = ys
+
+        def last_out(q, copy):
+            tp = psum.tile([P, OT, P], F32, name="tp")
+            oo = work.tile([P, OUT], F32, name="ooq", bufs=4)
+            for ot in range(OT):
+                nc.tensor.transpose(tp[:, ot, :], lys[q][:, ot, :], ident[:])
+            copy(out=oo[:], in_=tp[:].rearrange("p t o -> p (t o)"))
+            nc.sync.dma_start(out=out.rearrange("(c q p) o -> c q p o", q=Q, p=P)[CH - 1, q], in_=oo[:])
 
         widen(0)
-        for rh in range(2):
-            tp_x(0, rh)
-            exit_x(0, rh)
-        nc.vector.tensor_copy(out=w32[:, 0, :], in_=w_raw[0][:, :, D])
-        prep_w(0)
+        tp_x(0, 0)
+        exit_x(0, 0)
+        tp_x(0, 1)
+        exit_x(0, 1)
+        widen_w(0, 0, 2)
+        widen_w(0, 2, 4)
+        make_t(0, 0, 0, on_vector=True)
+        tp_w(0, 0)
+        exit_w(0, 0, nc.vector.tensor_copy)
+        make_t(0, 0, 2)
+        tp_w(0, 1)
+        exit_w(0, 1, nc.scalar.copy)
         quant_x(0)
         quant_w(0)
-        for t in range(T):
-            make_t(0, 0, t)
-        widen(1)
-        nc.vector.tensor_copy(out=w32[:, 1, :], in_=w_raw[1][:, :, D])
-        prep_w(1)
-        quant_w(1)
+        make_t(0, 0, 1, on_vector=True)
+        make_t(0, 0, 3)
+        widen_w(1, 0, 4)
 
-        for c in range(CH):
-            last = c == CH - 1
-            make_t(c, 1, 0)
-            if not last:
-                tp_x(c + 1, 0)
-                tp_x(c + 1, 1)
-                exit_x(c + 1, 0)
-            make_t(c, 1, 1)
-            if not last:
-                exit_x(c + 1, 1)
-            make_t(c, 1, 2)
-            make_t(c, 1, 3)
-            for q in range(Q):
-                mm_add(c, 0, q)
-                if c > 0 and q == 1:
-                    relu(c - 1, 1)
-                if c > 0 and q == 2:
-                    quant_h(c - 1, 1)
+        for c in range(CH - 1):
+            new_h(c)
+            stage1(c, 0, 0)
+            stage1(c, 0, 1)
+            if c == 0:
+                widen(1)
+                stage1(0, 0, 2)
+                stage1(0, 0, 3)
+                make_t(0, 1, 0)
+                tp_w(1, 0)
+                exit_w(1, 0, nc.scalar.copy)
+                tp_w(1, 1)
+                exit_w(1, 1, nc.scalar.copy)
+                make_t(0, 1, 1)
+                make_t(0, 1, 2)
+                make_t(0, 1, 3)
+                quant_w(1)
+            if c > 1:
+                exit_out(c - 2, 0)
+                exit_out(c - 2, 1)
+            for rh in range(2):
+                tp_x(c + 1, rh)
+                exit_x(c + 1, rh)
+            for t in range(T):
+                make_t(c + 1, 0, t)
+            if c > 0:
+                relu_chunk(c - 1)
+            if c > 0:
+                stage1(c, 0, 2)
+                quant_chunk(c - 1)
+                stage1(c, 0, 3)
             if c + 2 < CH:
                 widen(c + 2)
-            if c > 1:
-                out_half(c - 2, 0)
-                out_half(c - 2, 1)
-            if not last:
-                make_t(c + 1, 0, 0)
-                make_t(c + 1, 0, 1)
-            for q in range(Q):
-                mm_add(c, 1, q)
-                if q == 0 and not last:
-                    quant_x(c + 1)
-                if q == 1:
-                    relu(c, 0)
-                if q == 2:
-                    quant_h(c, 0)
-                    if c > 0:
-                        stage2(c - 1)
-                        tanh_y(c - 1, 0)
-                        tanh_y(c - 1, 1)
-            if not last:
-                make_t(c + 1, 0, 2)
-                make_t(c + 1, 0, 3)
-        relu(CH - 1, 1)
-        out_half(CH - 2, 0)
-        quant_h(CH - 1, 1)
-        out_half(CH - 2, 1)
-        stage2(CH - 1)
-        tanh_y(CH - 1, 0)
-        tanh_y(CH - 1, 1)
-        out_half(CH - 1, 0)
-        out_half(CH - 1, 1)
+            stage1(c, 1, 0)
+            quant_x(c + 1)
+            stage1(c, 1, 1)
+            if c > 0:
+                stage2(c - 1)
+                tanh_y(c - 1, 0)
+                tanh_y(c - 1, 1)
+            stage1(c, 1, 2)
+            stage1(c, 1, 3)
+            for t in range(T):
+                make_t(c + 1, 1, t, on_vector=(c == CH - 2 and t == 0))
+            if c > 0:
+                tp_out(c - 1, 0)
+                tp_out(c - 1, 1)
+
+        c = CH - 1
+        last_stage1(0, 0)
+        last_stage1(0, 1)
+        relu_chunk(c - 1, split=True)
+        exit_out(c - 2, 0)
+        exit_out(c - 2, 1)
+        last_stage1(1, 0)
+        last_relu(0)
+        last_stage1(1, 1)
+        quant_chunk(c - 1)
+        last_stage1(2, 0)
+        last_quant(0)
+        last_stage1(2, 1)
+        stage2(c - 1)
+        tanh_y(c - 1, 0)
+        tanh_y(c - 1, 1)
+        last_relu(1)
+        last_stage1(3, 0)
+        last_relu(2)
+        last_stage2(0)
+        last_quant(1)
+        last_stage1(3, 1)
+        last_quant(2)
+        tp_out(c - 1, 0)
+        exit_out(c - 1, 0)
+        tp_out(c - 1, 1)
+        exit_out(c - 1, 1)
+        last_relu(3)
+        last_stage2(1)
+        last_out(0, nc.scalar.copy)
+        last_quant(3)
+        last_stage2(2)
+        last_out(1, nc.vector.tensor_copy)
+        last_stage2(3)
+        last_out(2, nc.vector.tensor_copy)
+        last_out(3, nc.vector.tensor_copy)

@@ -27,6 +27,7 @@ CH = E // NE
 R = NE // P
 Q = NE // P
 OT = OUT // P
+RUN = 2
 W_PITCH = D + 16
 
 
@@ -46,6 +47,7 @@ def tile_edgenetwork_t_w4_kernel(tc, dst_feat, dst_hidden, src_feat, src_bytes, 
         b2c = [keep.tile([P, 2], BF16, name="b2c%d" % ot) for ot in range(OT)]
         w32 = keep.tile([P, G, T], F32)
         dummy = keep.tile([P, 1], F32)
+        warm = keep.tile([P, NE], BF16)
         w_codes = keep.tile([P, G, T, P], U32, align_bytes=64)
         w_scales = keep.tile([P, G, T, P], U8, align_bytes=64)
         w2 = keep.tile([P, G, 2 * OUT], U8, align_bytes=64)
@@ -76,6 +78,7 @@ def tile_edgenetwork_t_w4_kernel(tc, dst_feat, dst_hidden, src_feat, src_bytes, 
 
         nc.vector.memset(dummy[:], 0.0)
         nc.vector.memset(w2s[:].rearrange("p g n -> p (g n)").bitcast(I32), 0)
+        nc.gpsimd.memset(warm[:], 0.0)
         make_identity(nc, ident[:])
         load_x(0)
         nc.scalar.dma_start(out=sc_bc[:], in_=src_scale.rearrange("o k -> (o k)").partition_broadcast(P))
@@ -102,8 +105,8 @@ def tile_edgenetwork_t_w4_kernel(tc, dst_feat, dst_hidden, src_feat, src_bytes, 
         for c in range(4, CH):
             load_x(c)
 
-        def widen(c):
-            for r in range(R):
+        def widen(c, r0=0, r1=R):
+            for r in range(r0, r1):
                 nc.vector.tensor_tensor(
                     out=x_row[c][:, r, 2 * F + H : D],
                     in0=x_byt[c][:, r, :].bitcast(FP8),
@@ -195,7 +198,9 @@ def tile_edgenetwork_t_w4_kernel(tc, dst_feat, dst_hidden, src_feat, src_bytes, 
         h_tile = {}
         h_q = {}
 
-        def mm_add(c, g, q, h_out):
+        acc_ps = {}
+
+        def mm1(c, g, q):
             cols = slice(q * P, (q + 1) * P)
             xc, xs = x_q[c]
             acc = psum.tile([P, T, P], F32, name="acc", bufs=4)
@@ -209,10 +214,13 @@ def tile_edgenetwork_t_w4_kernel(tc, dst_feat, dst_hidden, src_feat, src_bytes, 
                     start=True,
                     stop=True,
                 )
+            acc_ps[c, g, q] = acc
+
+        def add_t(c, g, q, h_out):
             nc.vector.tensor_tensor(
-                out=h_out.rearrange("p (c i t) -> p c t i", i=4, t=T),
-                in0=acc[:].rearrange("p t (c i) -> p c t i", i=4),
-                in1=t_tile[c, g][:, :, cols].rearrange("p t (c i) -> p c t i", i=4),
+                out=h_out.rearrange("p (c i t) -> p c t i", i=RUN, t=T),
+                in0=acc_ps[c, g, q][:].rearrange("p t (c i) -> p c t i", i=RUN),
+                in1=t_tile[c, g][:, :, q * P : (q + 1) * P].rearrange("p t (c i) -> p c t i", i=RUN),
                 op=ALU.add,
             )
 
@@ -220,29 +228,31 @@ def tile_edgenetwork_t_w4_kernel(tc, dst_feat, dst_hidden, src_feat, src_bytes, 
             hh = work.tile([P, G, NE * T], BF16, name="hh", bufs=2, align_bytes=64)
             h_tile[c] = hh
 
-        def stage1(c, g, q):
-            mm_add(c, g, q, h_tile[c][:, g, q * P * T : (q + 1) * P * T])
+        def add1(c, g, q):
+            add_t(c, g, q, h_tile[c][:, g, q * P * T : (q + 1) * P * T])
 
         def relu(h):
             nc.vector.tensor_scalar(out=h, in0=h, scalar1=0.0, scalar2=None, op0=ALU.max)
 
-        def relu_chunk(c, split=False):
-            if split:
-                h = h_tile[c][:, 1, :]
+        def relu_half(c, g, on_scalar=False):
+            h = h_tile[c][:, g, :]
+            if on_scalar:
                 nc.scalar.activation(out=h, in_=h, func=ACT.Relu)
-                relu(h_tile[c][:, 0, :])
             else:
-                relu(h_tile[c][:].rearrange("p g w -> p (g w)"))
+                relu(h)
 
-        def quant_chunk(c):
-            hc = work.tile([P, G, NE], U32, name="hc", bufs=2, align_bytes=64)
-            hs = work.tile([P, G, NE], U8, name="hs", bufs=2, align_bytes=64)
-            h_q[c] = (hc, hs)
-            nc.vector.quantize_mx(
-                out=hc[:].rearrange("p g n -> p (g n)").bitcast(FP8X4),
-                scales=hs[:].rearrange("p g n -> p (g n)"),
-                in_=h_tile[c][:].rearrange("p g w -> p (g w)"),
-            )
+        def quant_half(c, g):
+            if g == 0:
+                hc = work.tile([P, G, NE], U32, name="hc", bufs=2, align_bytes=64)
+                hs = work.tile([P, G, NE], U8, name="hs", bufs=2, align_bytes=64)
+                h_q[c] = (hc, hs)
+            hc, hs = h_q[c]
+            nc.vector.quantize_mx(out=hc[:, g, :].bitcast(FP8X4), scales=hs[:, g, :], in_=h_tile[c][:, g, :])
+
+        def warm_up(n):
+            y = psum.tile([P, NE], F32, name="y", bufs=2)
+            for k in range(n):
+                nc.tensor.matmul(y[:], lhsT=warm[:, 0:P], rhs=warm[:], start=True, stop=True)
 
         y_ps = {}
         y_sb = {}
@@ -260,11 +270,10 @@ def tile_edgenetwork_t_w4_kernel(tc, dst_feat, dst_hidden, src_feat, src_bytes, 
                     stop=(g == G - 1),
                 )
 
-        def stage2(c):
-            for ot in range(OT):
-                y = psum.tile([P, NE], F32, name="y", bufs=2)
-                mm2(y[:], ot, *h_q[c])
-                y_ps[c, ot] = y
+        def stage2(c, ot):
+            y = psum.tile([P, NE], F32, name="y", bufs=2)
+            mm2(y[:], ot, *h_q[c])
+            y_ps[c, ot] = y
 
         def tanh_y(c, ot):
             ys = work.tile([P, NE], F32, name="ys", bufs=4)
@@ -287,11 +296,11 @@ def tile_edgenetwork_t_w4_kernel(tc, dst_feat, dst_hidden, src_feat, src_bytes, 
         hl = {}
         hl_q = {}
 
-        def last_stage1(q, g):
+        def last_add1(q, g):
             if g == 0:
                 hq = work.tile([P, G, P * T], BF16, name="hq", bufs=4, align_bytes=64)
                 hl[q] = hq
-            mm_add(CH - 1, g, q, hl[q][:, g, :])
+            add_t(CH - 1, g, q, hl[q][:, g, :])
 
         def last_relu(q):
             relu(hl[q][:].rearrange("p g w -> p (g w)"))
@@ -325,11 +334,13 @@ def tile_edgenetwork_t_w4_kernel(tc, dst_feat, dst_hidden, src_feat, src_bytes, 
             copy(out=oo[:], in_=tp[:].rearrange("p t o -> p (t o)"))
             nc.sync.dma_start(out=out.rearrange("(c q p) o -> c q p o", q=Q, p=P)[CH - 1, q], in_=oo[:])
 
+        warm_up(16)
         widen(0)
         tp_x(0, 0)
         exit_x(0, 0)
         tp_x(0, 1)
         exit_x(0, 1)
+        warm_up(2)
         widen_w(0, 0, 2)
         widen_w(0, 2, 4)
         make_t(0, 0, 0, on_vector=True)
@@ -338,82 +349,121 @@ def tile_edgenetwork_t_w4_kernel(tc, dst_feat, dst_hidden, src_feat, src_bytes, 
         make_t(0, 0, 2)
         tp_w(0, 1)
         exit_w(0, 1, nc.scalar.copy)
+        warm_up(1)
         quant_x(0)
         quant_w(0)
         make_t(0, 0, 1, on_vector=True)
         make_t(0, 0, 3)
         widen_w(1, 0, 4)
+        mm1(0, 0, 0)
+        mm1(0, 0, 1)
 
         for c in range(CH - 1):
             new_h(c)
-            stage1(c, 0, 0)
-            stage1(c, 0, 1)
+            mm1(c, 0, 2)
+            mm1(c, 0, 3)
             if c == 0:
-                widen(1)
-                stage1(0, 0, 2)
-                stage1(0, 0, 3)
+                add1(c, 0, 0)
                 make_t(0, 1, 0)
+                make_t(0, 1, 1)
                 tp_w(1, 0)
                 exit_w(1, 0, nc.scalar.copy)
                 tp_w(1, 1)
                 exit_w(1, 1, nc.scalar.copy)
-                make_t(0, 1, 1)
+                add1(c, 0, 1)
+                widen(1)
                 make_t(0, 1, 2)
                 make_t(0, 1, 3)
+                tp_x(c + 1, 0)
+                exit_x(c + 1, 0)
+                tp_x(c + 1, 1)
+                exit_x(c + 1, 1)
+                add1(c, 0, 2)
+                add1(c, 0, 3)
                 quant_w(1)
-            if c > 1:
-                exit_out(c - 2, 0)
-                exit_out(c - 2, 1)
-            for rh in range(2):
-                tp_x(c + 1, rh)
-                exit_x(c + 1, rh)
-            for t in range(T):
-                make_t(c + 1, 0, t)
+                for q in range(Q):
+                    mm1(c, 1, q)
+                for t in range(T):
+                    make_t(c + 1, 0, t)
+            else:
+                add1(c, 0, 0)
+                relu_half(c - 1, 0)
+                if c > 1:
+                    exit_out(c - 2, 0)
+                    exit_out(c - 2, 1)
+                make_t(c + 1, 0, 0)
+                tp_x(c + 1, 0)
+                exit_x(c + 1, 0)
+                mm1(c, 1, 0)
+                add1(c, 0, 1)
+                relu_half(c - 1, 1)
+                make_t(c + 1, 0, 1)
+                tp_x(c + 1, 1)
+                exit_x(c + 1, 1)
+                mm1(c, 1, 1)
+                add1(c, 0, 2)
+                quant_half(c - 1, 0)
+                mm1(c, 1, 2)
+                add1(c, 0, 3)
+                quant_half(c - 1, 1)
+                mm1(c, 1, 3)
+                make_t(c + 1, 0, 2)
+                make_t(c + 1, 0, 3)
+            make_t(c + 1, 1, 0, on_vector=(c == CH - 2))
+            make_t(c + 1, 1, 1)
+            make_t(c + 1, 1, 2)
             if c > 0:
-                relu_chunk(c - 1)
-            if c > 0:
-                stage1(c, 0, 2)
-                quant_chunk(c - 1)
-                stage1(c, 0, 3)
-            if c + 2 < CH:
-                widen(c + 2)
-            stage1(c, 1, 0)
-            quant_x(c + 1)
-            stage1(c, 1, 1)
-            if c > 0:
-                stage2(c - 1)
+                stage2(c - 1, 0)
                 tanh_y(c - 1, 0)
+                stage2(c - 1, 1)
                 tanh_y(c - 1, 1)
-            stage1(c, 1, 2)
-            stage1(c, 1, 3)
-            for t in range(T):
-                make_t(c + 1, 1, t, on_vector=(c == CH - 2 and t == 0))
+            add1(c, 1, 0)
+            if c + 2 < CH:
+                widen(c + 2, 0, 2)
+            add1(c, 1, 1)
+            quant_x(c + 1)
+            mm1(c + 1, 0, 0)
+            mm1(c + 1, 1 if c == CH - 2 else 0, 0 if c == CH - 2 else 1)
+            make_t(c + 1, 1, 3)
             if c > 0:
                 tp_out(c - 1, 0)
                 tp_out(c - 1, 1)
+            add1(c, 1, 2)
+            if c + 2 < CH:
+                widen(c + 2, 2, 4)
+            add1(c, 1, 3)
 
         c = CH - 1
-        last_stage1(0, 0)
-        last_stage1(0, 1)
-        relu_chunk(c - 1, split=True)
+        mm1(c, 0, 1)
+        mm1(c, 1, 1)
+        last_add1(0, 0)
+        relu_half(c - 1, 1, on_scalar=True)
+        relu_half(c - 1, 0)
+        mm1(c, 0, 2)
+        last_add1(0, 1)
+        mm1(c, 1, 2)
         exit_out(c - 2, 0)
         exit_out(c - 2, 1)
-        last_stage1(1, 0)
+        quant_half(c - 1, 0)
+        last_add1(1, 0)
+        mm1(c, 0, 3)
         last_relu(0)
-        last_stage1(1, 1)
-        quant_chunk(c - 1)
-        last_stage1(2, 0)
+        last_add1(1, 1)
+        mm1(c, 1, 3)
+        quant_half(c - 1, 1)
+        last_add1(2, 0)
         last_quant(0)
-        last_stage1(2, 1)
-        stage2(c - 1)
+        stage2(c - 1, 0)
         tanh_y(c - 1, 0)
+        stage2(c - 1, 1)
         tanh_y(c - 1, 1)
+        last_add1(2, 1)
         last_relu(1)
-        last_stage1(3, 0)
+        last_add1(3, 0)
         last_relu(2)
         last_stage2(0)
         last_quant(1)
-        last_stage1(3, 1)
+        last_add1(3, 1)
         last_quant(2)
         tp_out(c - 1, 0)
         exit_out(c - 1, 0)

from contextlib import ExitStack

import concourse.mybir as mybir
from concourse.masks import make_identity

E, F, H, MID, OUT = 4096, 64, 192, 1024, 256
D = 2 * (F + H)

F32 = mybir.dt.float32
BF16 = mybir.dt.bfloat16
I32 = mybir.dt.int32
U32 = mybir.dt.uint32
U8 = mybir.dt.uint8
FP8 = mybir.dt.float8_e4m3fn
FP8X4 = mybir.dt.float8_e4m3fn_x4
FP4X4 = mybir.dt.float4_e2m1fn_x4
ALU = mybir.AluOpType
ACT = mybir.ActivationFunctionType

FLOPS = 2 * E * (MID * (D + 1) + MID * OUT)

P = 128
T = 4
G = MID // 512
NE = 512
CH = E // NE
R = NE // P
Q = NE // P
OT = OUT // P
RUN = 2
W_PITCH = D + 16


def tile_edgenetwork_t_w4_kernel(tc, dst_feat, dst_hidden, src_feat, src_bytes, src_scale, edge_feat, W1, b1, W2_words, W2_scales, b2, out):
    nc = tc.nc
    with ExitStack() as ctx:
        keep = ctx.enter_context(tc.tile_pool(name="keep", bufs=1))
        xin = ctx.enter_context(tc.tile_pool(name="xin", bufs=CH))
        work = ctx.enter_context(tc.tile_pool(name="work", bufs=3))
        psum = ctx.enter_context(tc.psum_pool(name="psum", bufs=2))
        ctx.enter_context(tc.manual_schedule())

        ident = keep.tile([P, P], F32)
        sc_bc = keep.tile([P, H], F32)
        e_bc = keep.tile([P, E], BF16)
        b1c = keep.tile([P, G, T], BF16)
        b2c = [keep.tile([P, 2], BF16, name="b2c%d" % ot) for ot in range(OT)]
        w32 = keep.tile([P, G, T], F32)
        dummy = keep.tile([P, 1], F32)
        warm = keep.tile([P, NE], BF16)
        w_codes = keep.tile([P, G, T, P], U32, align_bytes=64)
        w_scales = keep.tile([P, G, T, P], U8, align_bytes=64)
        w2 = keep.tile([P, G, 2 * OUT], U8, align_bytes=64)
        w2s = keep.tile([P, G, OUT], U8, align_bytes=64)
        w_raw = [keep.tile([P, T, W_PITCH], BF16, name="w_raw%d" % g) for g in range(G)]

        x_row = {}
        x_byt = {}

        def load_x(c):
            xr = xin.tile([P, R, D], BF16, name="xr")
            xb = xin.tile([P, R, H], U8, name="xb")
            nc.sync.dma_start(out=xb[:], in_=src_bytes.rearrange("(c j r) f -> c j r f", j=P, r=R)[c])
            nc.sync.dma_start(out=xr[:, :, F : F + H], in_=dst_hidden.rearrange("(c j r) f -> c j r f", j=P, r=R)[c])
            nc.sync.dma_start(out=xr[:, :, 0:F], in_=dst_feat.rearrange("(c j r) f -> c j r f", j=P, r=R)[c])
            nc.sync.dma_start(out=xr[:, :, F + H : 2 * F + H], in_=src_feat.rearrange("(c j r) f -> c j r f", j=P, r=R)[c])
            x_row[c] = xr
            x_byt[c] = xb

        def load_w1(g, t0, t1):
            nc.sync.dma_start(
                out=w_raw[g][:, t0:t1, 0 : D + 1],
                in_=W1.rearrange("(g m t) k -> g m t k", g=G, t=T)[g][:, t0:t1, :],
            )

        def load_e(engine, c0, c1):
            engine.dma_start(out=e_bc[:, c0 * NE : c1 * NE], in_=edge_feat[c0 * NE : c1 * NE].partition_broadcast(P))

        nc.vector.memset(dummy[:], 0.0)
        nc.vector.memset(w2s[:].rearrange("p g n -> p (g n)").bitcast(I32), 0)
        nc.gpsimd.memset(warm[:], 0.0)
        make_identity(nc, ident[:])
        load_x(0)
        nc.scalar.dma_start(out=sc_bc[:], in_=src_scale.rearrange("o k -> (o k)").partition_broadcast(P))
        nc.scalar.dma_start(out=b1c[:], in_=b1.rearrange("(g m t) -> m g t", g=G, t=T))
        load_e(nc.scalar, 0, 1)
        nc.scalar.activation(out=dummy[:], in_=dummy[:], func=ACT.Tanh)
        load_w1(0, 0, 2)
        load_w1(0, 2, 4)
        load_w1(1, 0, 4)
        load_x(1)
        load_e(nc.sync, 1, 3)
        load_x(2)
        nc.sync.dma_start(out=w2[:], in_=W2_words.rearrange("g p n -> p g n"))
        for qd in range(4):
            nc.sync.dma_start(
                out=w2s[32 * qd : 32 * qd + 4, :, :].bitcast(I32),
                in_=W2_scales[:, 4 * qd : 4 * qd + 4, :].rearrange("g q n -> q g n").bitcast(I32),
            )
        with nc.allow_non_contiguous_dma(reason="256 bias values, one to a partition"):
            for ot in range(OT):
                nc.sync.dma_start(out=b2c[ot][:, 0:1], in_=b2.rearrange("(t p o) -> t p o", t=OT, o=1)[ot])
        load_x(3)
        load_e(nc.sync, 3, CH)
        for c in range(4, CH):
            load_x(c)

        def widen(c, r0=0, r1=R):
            for r in range(r0, r1):
                nc.vector.tensor_tensor(
                    out=x_row[c][:, r, 2 * F + H : D],
                    in0=x_byt[c][:, r, :].bitcast(FP8),
                    in1=sc_bc[:],
                    op=ALU.mult,
                )

        x_grp = {}
        x_tp = {}
        x_q = {}

        def tp_x(c, rh):
            tp = psum.tile([P, 4, P], F32, name="tp")
            words = x_row[c][:].rearrange("p r k -> p (r k)").bitcast(F32)
            for r2 in range(2):
                r = 2 * rh + r2
                for u in range(2):
                    nc.tensor.transpose(tp[:, 2 * r2 + u, :], words[:, 256 * r + u : 256 * (r + 1) : 2], ident[:])
            x_tp[c, rh] = tp

        def exit_x(c, rh):
            if rh == 0:
                xg = work.tile([P, NE * T], BF16, name="xg", bufs=2, align_bytes=64)
                x_grp[c] = xg
            dst = x_grp[c][:].bitcast(F32).rearrange("p (j h w) -> p j h w", h=2, w=4)[:, :, rh, :]
            nc.scalar.copy(out=dst, in_=x_tp[c, rh][:].rearrange("p w j -> p j w"))

        def quant_x(c):
            xc = work.tile([P, NE], U32, name="xc", bufs=2, align_bytes=64)
            xs = work.tile([P, NE], U8, name="xs", bufs=2, align_bytes=64)
            nc.vector.quantize_mx(out=xc[:].bitcast(FP8X4), scales=xs[:], in_=x_grp[c][:])
            x_q[c] = (xc, xs)

        w_grp = {}

        w_tp = {}

        def tp_w(g, h):
            words = w_raw[g][:].rearrange("p t k -> p (t k)").bitcast(F32)
            pitch = W_PITCH // 2
            tp = psum.tile([P, 4, P], F32, name="tp")
            for t2 in range(2):
                for u in range(2):
                    base = pitch * (2 * h + t2)
                    nc.tensor.transpose(tp[:, 2 * t2 + u, :], words[:, base + u : base + 256 : 2], ident[:])
            w_tp[g, h] = tp

        def exit_w(g, h, copy):
            if h == 0:
                wg = work.tile([P, T * P * 4], BF16, name="wg", bufs=2, align_bytes=64)
                w_grp[g] = wg
            dst = w_grp[g][:].bitcast(F32).rearrange("p (t m u) -> p t m u", t=T, u=2)[:, 2 * h : 2 * h + 2, :, :]
            copy(out=dst, in_=w_tp[g, h][:].rearrange("p (t u) m -> p t m u", u=2))

        def widen_w(g, t0, t1):
            nc.vector.tensor_copy(out=w32[:, g, t0:t1], in_=w_raw[g][:, t0:t1, D])

        def quant_w(g):
            nc.vector.quantize_mx(
                out=w_codes[:, g, :, :].rearrange("p t m -> p (t m)").bitcast(FP8X4),
                scales=w_scales[:, g, :, :].rearrange("p t m -> p (t m)"),
                in_=w_grp[g][:],
            )

        t_tile = {}

        def make_t(c, g, t, on_vector=False):
            if t == 0:
                tt = work.tile([P, T, NE], F32, name="tt", bufs=4)
                t_tile[c, g] = tt
            if on_vector:
                nc.vector.tensor_scalar(
                    out=t_tile[c, g][:, t, :],
                    in0=e_bc[:, c * NE : (c + 1) * NE],
                    scalar1=w_raw[g][:, t, D : D + 1],
                    scalar2=b1c[:, g, t : t + 1],
                    op0=ALU.mult,
                    op1=ALU.add,
                )
            else:
                nc.scalar.activation(
                    out=t_tile[c, g][:, t, :],
                    in_=e_bc[:, c * NE : (c + 1) * NE],
                    func=ACT.Identity,
                    bias=b1c[:, g, t : t + 1],
                    scale=w32[:, g, t : t + 1],
                )

        h_tile = {}
        h_q = {}

        acc_ps = {}

        def mm1(c, g, q):
            cols = slice(q * P, (q + 1) * P)
            xc, xs = x_q[c]
            acc = psum.tile([P, T, P], F32, name="acc", bufs=4)
            for t in range(T):
                nc.tensor.matmul_mx(
                    out=acc[:, t, :],
                    lhsT=w_codes[:, g, t, :].bitcast(FP8X4),
                    lhsT_scale=w_scales[:, g, t, :],
                    rhs=xc[:, cols].bitcast(FP8X4),
                    rhs_scale=xs[:, cols],
                    start=True,
                    stop=True,
                )
            acc_ps[c, g, q] = acc

        def add_t(c, g, q, h_out):
            nc.vector.tensor_tensor(
                out=h_out.rearrange("p (c i t) -> p c t i", i=RUN, t=T),
                in0=acc_ps[c, g, q][:].rearrange("p t (c i) -> p c t i", i=RUN),
                in1=t_tile[c, g][:, :, q * P : (q + 1) * P].rearrange("p t (c i) -> p c t i", i=RUN),
                op=ALU.add,
            )

        def new_h(c):
            hh = work.tile([P, G, NE * T], BF16, name="hh", bufs=2, align_bytes=64)
            h_tile[c] = hh

        def add1(c, g, q):
            add_t(c, g, q, h_tile[c][:, g, q * P * T : (q + 1) * P * T])

        def relu(h):
            nc.vector.tensor_scalar(out=h, in0=h, scalar1=0.0, scalar2=None, op0=ALU.max)

        def relu_half(c, g, on_scalar=False):
            h = h_tile[c][:, g, :]
            if on_scalar:
                nc.scalar.activation(out=h, in_=h, func=ACT.Relu)
            else:
                relu(h)

        def quant_half(c, g):
            if g == 0:
                hc = work.tile([P, G, NE], U32, name="hc", bufs=2, align_bytes=64)
                hs = work.tile([P, G, NE], U8, name="hs", bufs=2, align_bytes=64)
                h_q[c] = (hc, hs)
            hc, hs = h_q[c]
            nc.vector.quantize_mx(out=hc[:, g, :].bitcast(FP8X4), scales=hs[:, g, :], in_=h_tile[c][:, g, :])

        def warm_up(n):
            y = psum.tile([P, NE], F32, name="y", bufs=2)
            for k in range(n):
                nc.tensor.matmul(y[:], lhsT=warm[:, 0:P], rhs=warm[:], start=True, stop=True)

        y_ps = {}
        y_sb = {}
        o_ps = {}

        def mm2(y, ot, hc, hs):
            for g in range(G):
                nc.tensor.matmul_mx(
                    out=y,
                    lhsT=w2[:, g, 2 * P * ot : 2 * P * (ot + 1)].bitcast(FP4X4),
                    lhsT_scale=w2s[:, g, P * ot : P * (ot + 1)],
                    rhs=hc[:, g, :].bitcast(FP8X4),
                    rhs_scale=hs[:, g, :],
                    start=(g == 0),
                    stop=(g == G - 1),
                )

        def stage2(c, ot):
            y = psum.tile([P, NE], F32, name="y", bufs=2)
            mm2(y[:], ot, *h_q[c])
            y_ps[c, ot] = y

        def tanh_y(c, ot):
            ys = work.tile([P, NE], F32, name="ys", bufs=4)
            nc.scalar.activation(out=ys[:], in_=y_ps[c, ot][:], func=ACT.Tanh, bias=b2c[ot][:, 0:1], scale=1.0)
            y_sb[c, ot] = ys

        def tp_out(c, qh):
            tp = psum.tile([P, 4, P], F32, name="tp")
            for q2 in range(2):
                for ot in range(OT):
                    q = 2 * qh + q2
                    nc.tensor.transpose(tp[:, 2 * q2 + ot, :], y_sb[c, ot][:, q * P : (q + 1) * P], ident[:])
            o_ps[c, qh] = tp

        def exit_out(c, qh):
            oo = work.tile([P, 2, OUT], F32, name="oo", bufs=4)
            nc.scalar.copy(out=oo[:].rearrange("p q o -> p (q o)"), in_=o_ps[c, qh][:].rearrange("p w o -> p (w o)"))
            nc.sync.dma_start(out=out.rearrange("(c q p) o -> c p q o", q=Q, p=P)[c][:, 2 * qh : 2 * qh + 2, :], in_=oo[:])

        hl = {}
        hl_q = {}

        def last_add1(q, g):
            if g == 0:
                hq = work.tile([P, G, P * T], BF16, name="hq", bufs=4, align_bytes=64)
                hl[q] = hq
            add_t(CH - 1, g, q, hl[q][:, g, :])

        def last_relu(q):
            relu(hl[q][:].rearrange("p g w -> p (g w)"))

        def last_quant(q):
            hc = work.tile([P, G, P], U32, name="hcq", bufs=4, align_bytes=64)
            hs = work.tile([P, G, P], U8, name="hsq", bufs=4, align_bytes=64)
            nc.vector.quantize_mx(
                out=hc[:].rearrange("p g n -> p (g n)").bitcast(FP8X4),
                scales=hs[:].rearrange("p g n -> p (g n)"),
                in_=hl[q][:].rearrange("p g w -> p (g w)"),
            )
            hl_q[q] = (hc, hs)

        lys = {}

        def last_stage2(q):
            y = psum.tile([P, OT, P], F32, name="y", bufs=2)
            ys = work.tile([P, OT, P], F32, name="ysq")
            for ot in range(OT):
                mm2(y[:, ot, :], ot, *hl_q[q])
            for ot in range(OT):
                nc.scalar.activation(out=ys[:, ot, :], in_=y[:, ot, :], func=ACT.Tanh, bias=b2c[ot][:, 0:1], scale=1.0)
            lys[q] = ys

        def last_out(q, copy):
            tp = psum.tile([P, OT, P], F32, name="tp")
            oo = work.tile([P, OUT], F32, name="ooq", bufs=4)
            for ot in range(OT):
                nc.tensor.transpose(tp[:, ot, :], lys[q][:, ot, :], ident[:])
            copy(out=oo[:], in_=tp[:].rearrange("p t o -> p (t o)"))
            nc.sync.dma_start(out=out.rearrange("(c q p) o -> c q p o", q=Q, p=P)[CH - 1, q], in_=oo[:])

        warm_up(16)
        widen(0)
        tp_x(0, 0)
        exit_x(0, 0)
        tp_x(0, 1)
        exit_x(0, 1)
        warm_up(2)
        widen_w(0, 0, 2)
        widen_w(0, 2, 4)
        make_t(0, 0, 0, on_vector=True)
        tp_w(0, 0)
        exit_w(0, 0, nc.vector.tensor_copy)
        make_t(0, 0, 2)
        tp_w(0, 1)
        exit_w(0, 1, nc.scalar.copy)
        warm_up(1)
        quant_x(0)
        quant_w(0)
        make_t(0, 0, 1, on_vector=True)
        make_t(0, 0, 3)
        widen_w(1, 0, 4)
        mm1(0, 0, 0)
        mm1(0, 0, 1)

        for c in range(CH - 1):
            new_h(c)
            mm1(c, 0, 2)
            mm1(c, 0, 3)
            if c == 0:
                add1(c, 0, 0)
                make_t(0, 1, 0)
                make_t(0, 1, 1)
                tp_w(1, 0)
                exit_w(1, 0, nc.scalar.copy)
                tp_w(1, 1)
                exit_w(1, 1, nc.scalar.copy)
                add1(c, 0, 1)
                widen(1)
                make_t(0, 1, 2)
                make_t(0, 1, 3)
                tp_x(c + 1, 0)
                exit_x(c + 1, 0)
                tp_x(c + 1, 1)
                exit_x(c + 1, 1)
                add1(c, 0, 2)
                add1(c, 0, 3)
                quant_w(1)
                for q in range(Q):
                    mm1(c, 1, q)
                for t in range(T):
                    make_t(c + 1, 0, t)
            else:
                add1(c, 0, 0)
                relu_half(c - 1, 0)
                if c > 1:
                    exit_out(c - 2, 0)
                    exit_out(c - 2, 1)
                make_t(c + 1, 0, 0)
                tp_x(c + 1, 0)
                exit_x(c + 1, 0)
                mm1(c, 1, 0)
                add1(c, 0, 1)
                relu_half(c - 1, 1)
                make_t(c + 1, 0, 1)
                tp_x(c + 1, 1)
                exit_x(c + 1, 1)
                mm1(c, 1, 1)
                add1(c, 0, 2)
                quant_half(c - 1, 0)
                mm1(c, 1, 2)
                add1(c, 0, 3)
                quant_half(c - 1, 1)
                mm1(c, 1, 3)
                make_t(c + 1, 0, 2)
                make_t(c + 1, 0, 3)
            make_t(c + 1, 1, 0, on_vector=(c == CH - 2))
            make_t(c + 1, 1, 1)
            make_t(c + 1, 1, 2)
            if c > 0:
                stage2(c - 1, 0)
                tanh_y(c - 1, 0)
                stage2(c - 1, 1)
                tanh_y(c - 1, 1)
            add1(c, 1, 0)
            if c + 2 < CH:
                widen(c + 2, 0, 2)
            add1(c, 1, 1)
            quant_x(c + 1)
            mm1(c + 1, 0, 0)
            mm1(c + 1, 1 if c == CH - 2 else 0, 0 if c == CH - 2 else 1)
            make_t(c + 1, 1, 3)
            if c > 0:
                tp_out(c - 1, 0)
                tp_out(c - 1, 1)
            add1(c, 1, 2)
            if c + 2 < CH:
                widen(c + 2, 2, 4)
            add1(c, 1, 3)

        c = CH - 1
        mm1(c, 0, 1)
        mm1(c, 1, 1)
        last_add1(0, 0)
        relu_half(c - 1, 1, on_scalar=True)
        relu_half(c - 1, 0)
        mm1(c, 0, 2)
        last_add1(0, 1)
        mm1(c, 1, 2)
        exit_out(c - 2, 0)
        exit_out(c - 2, 1)
        quant_half(c - 1, 0)
        last_add1(1, 0)
        mm1(c, 0, 3)
        last_relu(0)
        last_add1(1, 1)
        mm1(c, 1, 3)
        quant_half(c - 1, 1)
        last_add1(2, 0)
        last_quant(0)
        stage2(c - 1, 0)
        tanh_y(c - 1, 0)
        stage2(c - 1, 1)
        tanh_y(c - 1, 1)
        last_add1(2, 1)
        last_relu(1)
        last_add1(3, 0)
        last_relu(2)
        last_stage2(0)
        last_quant(1)
        last_add1(3, 1)
        last_quant(2)
        tp_out(c - 1, 0)
        exit_out(c - 1, 0)
        tp_out(c - 1, 1)
        exit_out(c - 1, 1)
        last_relu(3)
        last_stage2(1)
        last_out(0, nc.scalar.copy)
        last_quant(3)
        last_stage2(2)
        last_out(1, nc.vector.tensor_copy)
        last_stage2(3)
        last_out(2, nc.vector.tensor_copy)
        last_out(3, nc.vector.tensor_copy)
